import numpy as np
import ml_dtypes


def mxq(x, axis, fmt="e4m3"):
    dtype, down = {"e4m3": (ml_dtypes.float8_e4m3fn, 7), "e5m2": (ml_dtypes.float8_e5m2, 14)}[fmt]
    v = np.moveaxis(np.asarray(x, np.float32).astype(ml_dtypes.bfloat16).astype(np.float64), axis, -1)
    blocks = v.reshape(v.shape[:-1] + (-1, 32))
    amax = np.abs(blocks).max(-1, keepdims=True)
    byte = np.maximum(np.where(amax > 0, np.frexp(amax)[1] - 1 + 127, 0) - down, 1)
    scale = np.exp2(byte - 127.0)
    codes = (blocks / scale).astype(np.float32).astype(dtype).astype(np.float64)
    return np.moveaxis((codes * scale).reshape(v.shape), -1, axis)


WIDE = False


def mx_kscale(k):
    if not WIDE:
        return np.ones(k)
    levels = np.array([10, -10, 5, -5, 0])
    if k % 512:
        return np.exp2(np.random.permutation(np.resize(levels, k // 32))).repeat(32)
    a = np.empty((k // 512, 16))
    for p in range(k // 512):
        a[p, :8] = np.random.permutation(np.resize(levels, 8))
        for g in range(8):
            far = levels[np.abs(levels - a[p, g]) >= 10]
            a[p, g + 8] = far[np.random.randint(len(far))]
    return np.exp2(a.ravel()).repeat(32)


BF16 = ml_dtypes.bfloat16


def bf(x):
    return np.asarray(x, np.float32).astype(BF16)


def f64(x):
    return np.asarray(x).astype(np.float64)


B, N, D, BD = 4, 1024, 512, 512


def setup_inputs():
    s, u = mx_kscale(D), mx_kscale(D)
    t = mx_kscale(BD)
    return {
        "keys": bf(np.random.standard_normal((B, N, D)) * s),
        "values": bf(np.random.standard_normal((B, N, D)) * u),
        "Wbk": bf(np.random.standard_normal((BD, D)) / np.sqrt(D) / s[None, :]),
        "bbk": bf(np.random.standard_normal(BD) * 0.1),
        "Wbv": bf(np.random.standard_normal((BD, D)) / np.sqrt(D) / u[None, :] * t[:, None]),
        "bbv": bf(np.random.standard_normal(BD) * 0.1 * t),
        "Wbc": bf(np.random.standard_normal((D, BD)) / np.sqrt(BD) / t[None, :]),
        "bbc": bf(np.random.standard_normal(D) * 0.1),
    }


def reference(keys, values, Wbk, bbk, Wbv, bbv, Wbc, bbc):
    k = (mxq(f64(keys), 2, "e4m3") @ mxq(f64(Wbk), 1, "e4m3").T) + f64(bbk)
    v = (mxq(f64(values), 2, "e4m3") @ mxq(f64(Wbv), 1, "e4m3").T) + f64(bbv)
    return (mxq(k * v, 2, "e4m3") @ mxq(f64(Wbc), 1, "e4m3").T) + f64(bbc)

@@ -1,0 +1,275 @@
+from contextlib import ExitStack
+
+import concourse.mybir as mybir
+from concourse.masks import make_identity
+
+F32 = mybir.dt.float32
+BF16 = mybir.dt.bfloat16
+U32 = mybir.dt.uint32
+U8 = mybir.dt.uint8
+FP8X4 = mybir.dt.float8_e4m3fn_x4
+ADD = mybir.AluOpType.add
+MULT = mybir.AluOpType.mult
+IDENTITY = mybir.ActivationFunctionType.Identity
+
+P = 128
+PACK = 4
+WIDTH = P * PACK
+BLOCK = 512
+TILES = BLOCK // P
+TOKENS = 4 * 1024
+CHUNKS = TOKENS // BLOCK
+VECTOR_REGROUPS = 64
+
+FLOPS = 3 * 2 * TOKENS * WIDTH * WIDTH
+
+PAIRS = "r (i q u) -> r i u q"
+
+
+def tile_learnedbindingmemory_pa_t_kernel(
+    tc, keys, values, Wbk, bbk, Wbv, bbv, Wbc, bbc, out
+):
+    nc = tc.nc
+    key_rows = keys.flatten_outer_dims()
+    value_rows = values.flatten_outer_dims()
+    out_rows = out.flatten_outer_dims()
+
+    with ExitStack() as ctx:
+        fixed = ctx.enter_context(tc.tile_pool(name="fixed", bufs=1))
+        ring = ctx.enter_context(tc.tile_pool(name="ring", bufs=2))
+        psum = ctx.enter_context(tc.psum_pool(name="psum", bufs=2))
+
+        raw = {}
+        turned = {}
+        grouped = {}
+        codes = {}
+        scales = {}
+        projected = {}
+        planes = {}
+        combined = {}
+
+        def load(block, rows, view):
+            raw[block] = fixed.tile([P, TILES * WIDTH], BF16, name="raw_%s_%s" % block)
+            nc.sync.dma_start(
+                out=raw[block][:].rearrange("r (i d) -> r i d", i=TILES),
+                in_=rows.rearrange(view, i=TILES),
+            )
+
+        def chunk_of(rows, c):
+            return rows[c * BLOCK : (c + 1) * BLOCK, :]
+
+        NEIGHBOURS = "(r i) d -> r i d"
+        STRIPES = "(i r) d -> r i d"
+
+        bias_k16 = fixed.tile([P, PACK], BF16)
+        bias_v16 = fixed.tile([P, PACK], BF16)
+        bias_row = fixed.tile([P, WIDTH], BF16)
+        ones = fixed.tile([P, P], BF16)
+        nc.vector.memset(bias_row[:], 0.0)
+        nc.vector.memset(ones[:], 1.0)
+        nc.scalar.dma_start(out=bias_k16[:], in_=bbk.rearrange("(r t) -> r t", t=PACK))
+        nc.scalar.dma_start(out=bias_v16[:], in_=bbv.rearrange("(r t) -> r t", t=PACK))
+        nc.scalar.dma_start(out=bias_row[0:1, :], in_=bbc.unsqueeze(0))
+
+        load(("wk", 0), Wbk, NEIGHBOURS)
+        load(("k", 0), chunk_of(key_rows, 0), NEIGHBOURS)
+        load(("wv", 0), Wbv, NEIGHBOURS)
+        load(("v", 0), chunk_of(value_rows, 0), NEIGHBOURS)
+        load(("k", 1), chunk_of(key_rows, 1), NEIGHBOURS)
+        load(("v", 1), chunk_of(value_rows, 1), NEIGHBOURS)
+        load(("wc", 0), Wbc, STRIPES)
+        for c in range(2, CHUNKS):
+            load(("k", c), chunk_of(key_rows, c), NEIGHBOURS)
+            load(("v", c), chunk_of(value_rows, c), NEIGHBOURS)
+
+        identity = fixed.tile([P, P], F32)
+        make_identity(nc, identity[:])
+
+        bias_k = fixed.tile([P, PACK], F32)
+        bias_v = fixed.tile([P, PACK], F32)
+        nc.scalar.activation(out=bias_k[:], in_=bias_k16[:], func=IDENTITY)
+        nc.scalar.activation(out=bias_v[:], in_=bias_v16[:], func=IDENTITY)
+
+        def transpose(block, bank_tag="turned", word_order=PAIRS):
+            words = raw[block][:].bitcast(F32).rearrange(word_order, i=TILES, u=2)
+            for half in range(2):
+                bank = psum.tile([P, 2, 2, P], F32, name="turned", tag=bank_tag)
+                for j in range(2):
+                    for u in range(2):
+                        nc.tensor.transpose(
+                            bank[:, j, u, :], words[:, 2 * half + j, u, :], identity[:]
+                        )
+                turned[(block, half)] = bank
+
+        def gather(block, copies):
+            grouped[block] = ring.tile(
+                [P, BLOCK * PACK], BF16, name="grouped", tag="grouped", bufs=4, align_bytes=64
+            )
+            pairs = grouped[block][:].bitcast(F32).rearrange("q (i n u) -> q i n u", i=TILES, u=2)
+            for half in range(2):
+                copies[half](
+                    out=pairs[:, 2 * half : 2 * half + 2],
+                    in_=turned[(block, half)][:].rearrange("q j u n -> q j n u"),
+                )
+
+        def packed_tiles(block, pool):
+            kind = block[0]
+            codes[block] = pool.tile(
+                [P, BLOCK], U32, name="codes_%s_%s" % block, tag="codes_%s" % kind, align_bytes=64
+            )
+            scales[block] = pool.tile(
+                [P, BLOCK], U8, name="scales_%s_%s" % block, tag="scales_%s" % kind, align_bytes=64
+            )
+
+        def quantise(block, pool):
+            packed_tiles(block, pool)
+            nc.vector.quantize_mx(
+                out=codes[block][:].bitcast(FP8X4), scales=scales[block][:], in_=grouped[block][:]
+            )
+
+        BY_SCALAR = (nc.scalar.copy, nc.scalar.copy)
+        BY_VECTOR = (nc.vector.tensor_copy, nc.vector.tensor_copy)
+        BY_BOTH = (nc.scalar.copy, nc.vector.tensor_copy)
+
+        def prepare(block, pool, bank_tag, copies, word_order=PAIRS):
+            transpose(block, bank_tag, word_order)
+            gather(block, copies)
+            quantise(block, pool)
+
+        def project(stream, c, t):
+            weight = ("w" + stream, 0)
+            features = slice(t * P, (t + 1) * P)
+            bank = psum.tile([P, BLOCK], F32, name="projected", tag="projected_%s" % stream)
+            nc.tensor.matmul_mx(
+                out=bank[:],
+                lhsT=codes[weight][:, features].bitcast(FP8X4),
+                lhsT_scale=scales[weight][:, features],
+                rhs=codes[(stream, c)][:].bitcast(FP8X4),
+                rhs_scale=scales[(stream, c)][:],
+                start=True,
+                stop=True,
+            )
+            projected[(stream, c, t)] = bank
+
+        def project_pair(c, first):
+            for stream in ("k", "v"):
+                project(stream, c, first)
+                project(stream, c, first + 1)
+
+        def bind(c, t):
+            if t == 0:
+                planes[c] = ring.tile([P, PACK, BLOCK], BF16, name="planes", tag="planes", bufs=3)
+            k_biased = ring.tile([P, BLOCK], F32, name="k_biased", tag="k_biased", bufs=4)
+            nc.scalar.activation(
+                out=k_biased[:], in_=projected[("k", c, t)][:], func=IDENTITY,
+                bias=bias_k[:, t : t + 1], scale=1.0,
+            )
+            nc.vector.scalar_tensor_tensor(
+                out=planes[c][:, t, :], in0=projected[("v", c, t)][:], scalar=bias_v[:, t : t + 1],
+                in1=k_biased[:], op0=ADD, op1=MULT,
+            )
+
+        def regroup(copy, c, first, last):
+            by_token = grouped[("p", c)][:].rearrange("r (n t) -> r n t", t=PACK)
+            copy(
+                out=by_token[:, first:last, :].rearrange("r (m s) t -> r m t s", s=4),
+                in_=planes[c][:, :, first:last].rearrange("r t (m s) -> r m t s", s=4),
+            )
+
+        def quantise_product(c, half):
+            product = ("p", c)
+            if half == 0:
+                grouped[product] = ring.tile(
+                    [P, BLOCK * PACK], BF16, name="grouped_p", tag="grouped_p", align_bytes=64
+                )
+                packed_tiles(product, ring)
+            first, last = half * 2 * P, (half + 1) * 2 * P
+            regroup(nc.scalar.copy, c, first, first + P)
+            if half == 0:
+                regroup(nc.scalar.copy, c, first + P, last)
+            else:
+                regroup(nc.scalar.copy, c, first + P, last - VECTOR_REGROUPS)
+                regroup(nc.vector.tensor_copy, c, last - VECTOR_REGROUPS, last)
+            nc.vector.quantize_mx(
+                out=codes[product][:, first:last].bitcast(FP8X4),
+                scales=scales[product][:, first:last],
+                in_=grouped[product][:, first * PACK : last * PACK],
+            )
+
+        def combine(c, i):
+            tokens = slice(i * P, (i + 1) * P)
+            bank = psum.tile([P, WIDTH], F32, name="combined", tag="combined")
+            nc.tensor.matmul_mx(
+                out=bank[:],
+                lhsT=codes[("p", c)][:, tokens].bitcast(FP8X4),
+                lhsT_scale=scales[("p", c)][:, tokens],
+                rhs=codes[("wc", 0)][:].bitcast(FP8X4),
+                rhs_scale=scales[("wc", 0)][:],
+                start=True,
+                stop=True,
+            )
+            combined[(c, i)] = bank
+
+        def finish(c, i):
+            result = ring.tile([P, WIDTH], F32, name="result", tag="result", bufs=6)
+            nc.vector.tensor_tensor(out=result[:], in0=combined[(c, i)][:], in1=bias_c[:], op=ADD)
+            nc.sync.dma_start(
+                out=chunk_of(out_rows, c).rearrange(NEIGHBOURS, i=TILES)[:, i, :], in_=result[:]
+            )
+
+        bias_c = fixed.tile([P, WIDTH], F32)
+
+        def spread_bias_c():
+            spread = psum.tile([P, WIDTH], F32, name="spread", tag="combined")
+            nc.tensor.matmul(out=spread[:], lhsT=ones[:], rhs=bias_row[:], start=True, stop=True)
+            nc.vector.tensor_copy(out=bias_c[:], in_=spread[:])
+
+        prepare(("wk", 0), fixed, "projected_k", BY_BOTH)
+        prepare(("k", 0), ring, "turned", BY_BOTH)
+        prepare(("wv", 0), fixed, "projected_v", BY_BOTH)
+        prepare(("v", 0), ring, "combined", BY_BOTH)
+        transpose(("k", 1))
+        project_pair(0, 0)
+        gather(("k", 1), BY_SCALAR)
+        transpose(("v", 1))
+
+        live = range(CHUNKS)
+        for a in range(CHUNKS + 2):
+            if a in live:
+                bind(a, 0)
+                bind(a, 1)
+            if a - 2 in live:
+                combine(a - 2, 2)
+                combine(a - 2, 3)
+            if a in live:
+                project_pair(a, 2)
+            if a + 1 in live:
+                quantise(("k", a + 1), ring)
+            if a - 1 in live:
+                quantise_product(a - 1, 0)
+            if a - 2 in live:
+                finish(a - 2, 2)
+                finish(a - 2, 3)
+            if a + 1 in live:
+                gather(("v", a + 1), BY_SCALAR)
+                quantise(("v", a + 1), ring)
+            if a + 2 in live:
+                transpose(("k", a + 2))
+            if a - 1 in live:
+                combine(a - 1, 0)
+                combine(a - 1, 1)
+            if a in live:
+                bind(a, 2)
+                bind(a, 3)
+            if a == 0:
+                spread_bias_c()
+                prepare(("wc", 0), fixed, "combined", BY_VECTOR, PAIRS)
+            if a + 1 in live:
+                project_pair(a + 1, 0)
+            if a - 1 in live:
+                quantise_product(a - 1, 1)
+                finish(a - 1, 0)
+                finish(a - 1, 1)
+            if a + 2 in live:
+                gather(("k", a + 2), BY_SCALAR)
+                transpose(("v", a + 2))

@@ -19,7 +19,6 @@ BLOCK = 512
 TILES = BLOCK // P
 TOKENS = 4 * 1024
 CHUNKS = TOKENS // BLOCK
-VECTOR_REGROUPS = 64
 
 FLOPS = 3 * 2 * TOKENS * WIDTH * WIDTH
 
@@ -176,20 +175,25 @@ def tile_learnedbindingmemory_pa_t_kernel(
                 in_=planes[c][:, :, first:last].rearrange("r t (m s) -> r m t s", s=4),
             )
 
+        def regroup_by_gpsimd(c, first, last):
+            by_token = grouped[("p", c)][:].rearrange("r (n t) -> r n t", t=PACK)
+            nc.gpsimd.tensor_scalar(
+                out=by_token[:, first:last, :],
+                in0=planes[c][:, :, first:last].rearrange("r t n -> r n t"),
+                scalar1=1.0, scalar2=0.0, op0=MULT, op1=ADD,
+            )
+
         def quantise_product(c, half):
             product = ("p", c)
+            first, last = half * 2 * P, (half + 1) * 2 * P
             if half == 0:
                 grouped[product] = ring.tile(
                     [P, BLOCK * PACK], BF16, name="grouped_p", tag="grouped_p", align_bytes=64
                 )
                 packed_tiles(product, ring)
-            first, last = half * 2 * P, (half + 1) * 2 * P
-            regroup(nc.scalar.copy, c, first, first + P)
-            if half == 0:
+                regroup_by_gpsimd(c, 2 * P, 4 * P)
+                regroup(nc.scalar.copy, c, first, first + P)
                 regroup(nc.scalar.copy, c, first + P, last)
-            else:
-                regroup(nc.scalar.copy, c, first + P, last - VECTOR_REGROUPS)
-                regroup(nc.vector.tensor_copy, c, last - VECTOR_REGROUPS, last)
             nc.vector.quantize_mx(
                 out=codes[product][:, first:last].bitcast(FP8X4),
                 scales=scales[product][:, first:last],

@@ -19,10 +19,10 @@ BLOCK = 512
 TILES = BLOCK // P
 TOKENS = 4 * 1024
 CHUNKS = TOKENS // BLOCK
+HALF = BLOCK // 2
+GPSIMD_REGROUPS = 256
 
 FLOPS = 3 * 2 * TOKENS * WIDTH * WIDTH
-
-PAIRS = "r (i q u) -> r i u q"
 
 
 def tile_learnedbindingmemory_pa_t_kernel(
@@ -34,32 +34,56 @@ def tile_learnedbindingmemory_pa_t_kernel(
     out_rows = out.flatten_outer_dims()
 
     with ExitStack() as ctx:
+        ctx.enter_context(tc.manual_schedule())
         fixed = ctx.enter_context(tc.tile_pool(name="fixed", bufs=1))
-        ring = ctx.enter_context(tc.tile_pool(name="ring", bufs=2))
-        psum = ctx.enter_context(tc.psum_pool(name="psum", bufs=2))
+        ring = ctx.enter_context(tc.tile_pool(name="ring", bufs=3))
+        psum = ctx.enter_context(tc.psum_pool(name="psum", bufs=4))
 
+        live = range(CHUNKS)
         raw = {}
         turned = {}
         grouped = {}
         codes = {}
         scales = {}
         projected = {}
+        biased = {}
         planes = {}
         combined = {}
-
-        def load(block, rows, view):
-            raw[block] = fixed.tile([P, TILES * WIDTH], BF16, name="raw_%s_%s" % block)
-            nc.sync.dma_start(
-                out=raw[block][:].rearrange("r (i d) -> r i d", i=TILES),
-                in_=rows.rearrange(view, i=TILES),
-            )
-
-        def chunk_of(rows, c):
-            return rows[c * BLOCK : (c + 1) * BLOCK, :]
 
         NEIGHBOURS = "(r i) d -> r i d"
         STRIPES = "(i r) d -> r i d"
 
+        def rows_of(block):
+            kind, c = block
+            if kind in ("k", "v"):
+                rows = key_rows if kind == "k" else value_rows
+                return rows[c * BLOCK : (c + 1) * BLOCK, :].rearrange(NEIGHBOURS, i=TILES)
+            if kind == "wc":
+                return Wbc.rearrange(STRIPES, i=TILES)
+            return (Wbk if kind == "wk" else Wbv).rearrange(NEIGHBOURS, i=TILES)
+
+        def load(block):
+            tile = fixed.tile([P, TILES * WIDTH], BF16, name="raw_%s_%s" % block)
+            nc.sync.dma_start(out=tile[:].rearrange("r (i d) -> r i d", i=TILES), in_=rows_of(block))
+            for half in range(2):
+                raw[(block, half)] = tile[:, half * 2 * WIDTH : (half + 1) * 2 * WIDTH]
+
+        def load_half(block, half):
+            tile = fixed.tile([P, 2 * WIDTH], BF16, name="raw_%s_%s_half%s" % (block + (half,)))
+            nc.sync.dma_start(
+                out=tile[:].rearrange("r (j d) -> r j d", j=2),
+                in_=rows_of(block)[:, 2 * half : 2 * half + 2, :],
+            )
+            raw[(block, half)] = tile[:]
+
+        WK, WV, WC = ("wk", 0), ("wv", 0), ("wc", 0)
+        first_halves = [
+            (WK, 0), (("k", 0), 0), (("k", 0), 1), (WV, 0), (("v", 0), 0), (("v", 0), 1),
+            (WK, 1), (WV, 1),
+        ]
+
+        identity = fixed.tile([P, P], F32)
+        make_identity(nc, identity[:])
         bias_k16 = fixed.tile([P, PACK], BF16)
         bias_v16 = fixed.tile([P, PACK], BF16)
         bias_row = fixed.tile([P, WIDTH], BF16)
@@ -70,48 +94,50 @@ def tile_learnedbindingmemory_pa_t_kernel(
         nc.scalar.dma_start(out=bias_v16[:], in_=bbv.rearrange("(r t) -> r t", t=PACK))
         nc.scalar.dma_start(out=bias_row[0:1, :], in_=bbc.unsqueeze(0))
 
-        load(("wk", 0), Wbk, NEIGHBOURS)
-        load(("k", 0), chunk_of(key_rows, 0), NEIGHBOURS)
-        load(("wv", 0), Wbv, NEIGHBOURS)
-        load(("v", 0), chunk_of(value_rows, 0), NEIGHBOURS)
-        load(("k", 1), chunk_of(key_rows, 1), NEIGHBOURS)
-        load(("v", 1), chunk_of(value_rows, 1), NEIGHBOURS)
-        load(("wc", 0), Wbc, STRIPES)
+        for block, half in first_halves:
+            load_half(block, half)
+        load(("k", 1))
+        load(("v", 1))
+        load(WC)
         for c in range(2, CHUNKS):
-            load(("k", c), chunk_of(key_rows, c), NEIGHBOURS)
-            load(("v", c), chunk_of(value_rows, c), NEIGHBOURS)
-
-        identity = fixed.tile([P, P], F32)
-        make_identity(nc, identity[:])
+            load(("k", c))
+            load(("v", c))
 
         bias_k = fixed.tile([P, PACK], F32)
         bias_v = fixed.tile([P, PACK], F32)
         nc.scalar.activation(out=bias_k[:], in_=bias_k16[:], func=IDENTITY)
         nc.scalar.activation(out=bias_v[:], in_=bias_v16[:], func=IDENTITY)
 
-        def transpose(block, bank_tag="turned", word_order=PAIRS):
-            words = raw[block][:].bitcast(F32).rearrange(word_order, i=TILES, u=2)
-            for half in range(2):
-                bank = psum.tile([P, 2, 2, P], F32, name="turned", tag=bank_tag)
-                for j in range(2):
-                    for u in range(2):
-                        nc.tensor.transpose(
-                            bank[:, j, u, :], words[:, 2 * half + j, u, :], identity[:]
-                        )
-                turned[(block, half)] = bank
+        FOR_SCALAR, FOR_VECTOR = "for_scalar", "for_vector"
 
-        def gather(block, copies):
-            grouped[block] = ring.tile(
-                [P, BLOCK * PACK], BF16, name="grouped", tag="grouped", bufs=4, align_bytes=64
-            )
-            pairs = grouped[block][:].bitcast(F32).rearrange("q (i n u) -> q i n u", i=TILES, u=2)
-            for half in range(2):
-                copies[half](
-                    out=pairs[:, 2 * half : 2 * half + 2],
-                    in_=turned[(block, half)][:].rearrange("q j u n -> q j n u"),
+        def exists(block):
+            return block[0] not in ("k", "v") or block[1] in live
+
+        def transpose(block, half, emptied=FOR_SCALAR):
+            if not exists(block):
+                return
+            words = raw[(block, half)].bitcast(F32).rearrange("r (j q u) -> r j u q", j=2, u=2)
+            bank = psum.tile([P, 2, 2, P], F32, name="turned", tag=emptied)
+            for j in range(2):
+                for u in range(2):
+                    nc.tensor.transpose(bank[:, j, u, :], words[:, j, u, :], identity[:])
+            turned[(block, half)] = bank
+
+        def gather(block, half, copy=nc.scalar.copy):
+            if not exists(block):
+                return
+            if half == 0:
+                grouped[block] = ring.tile(
+                    [P, BLOCK * PACK], BF16, name="grouped", tag="grouped", bufs=6, align_bytes=64
                 )
+            pairs = grouped[block][:].bitcast(F32).rearrange("q (i n u) -> q i n u", i=TILES, u=2)
+            copy(
+                out=pairs[:, 2 * half : 2 * half + 2],
+                in_=turned[(block, half)][:].rearrange("q j u n -> q j n u"),
+            )
 
-        def packed_tiles(block, pool):
+        def packed_tiles(block):
+            pool = fixed if block in (WK, WV, WC) else ring
             kind = block[0]
             codes[block] = pool.tile(
                 [P, BLOCK], U32, name="codes_%s_%s" % block, tag="codes_%s" % kind, align_bytes=64
@@ -120,25 +146,25 @@ def tile_learnedbindingmemory_pa_t_kernel(
                 [P, BLOCK], U8, name="scales_%s_%s" % block, tag="scales_%s" % kind, align_bytes=64
             )
 
-        def quantise(block, pool):
-            packed_tiles(block, pool)
+        def quantise_rows(block, first, last):
             nc.vector.quantize_mx(
-                out=codes[block][:].bitcast(FP8X4), scales=scales[block][:], in_=grouped[block][:]
+                out=codes[block][:, first:last].bitcast(FP8X4),
+                scales=scales[block][:, first:last],
+                in_=grouped[block][:, first * PACK : last * PACK],
             )
 
-        BY_SCALAR = (nc.scalar.copy, nc.scalar.copy)
-        BY_VECTOR = (nc.vector.tensor_copy, nc.vector.tensor_copy)
-        BY_BOTH = (nc.scalar.copy, nc.vector.tensor_copy)
-
-        def prepare(block, pool, bank_tag, copies, word_order=PAIRS):
-            transpose(block, bank_tag, word_order)
-            gather(block, copies)
-            quantise(block, pool)
+        def quantise(block):
+            if exists(block):
+                packed_tiles(block)
+                quantise_rows(block, 0, BLOCK)
 
         def project(stream, c, t):
-            weight = ("w" + stream, 0)
+            if c not in live:
+                return
+            weight = WK if stream == "k" else WV
             features = slice(t * P, (t + 1) * P)
-            bank = psum.tile([P, BLOCK], F32, name="projected", tag="projected_%s" % stream)
+            emptied = FOR_SCALAR if stream == "k" else FOR_VECTOR
+            bank = psum.tile([P, BLOCK], F32, name="projected", tag=emptied)
             nc.tensor.matmul_mx(
                 out=bank[:],
                 lhsT=codes[weight][:, features].bitcast(FP8X4),
@@ -150,32 +176,45 @@ def tile_learnedbindingmemory_pa_t_kernel(
             )
             projected[(stream, c, t)] = bank
 
-        def project_pair(c, first):
-            for stream in ("k", "v"):
-                project(stream, c, first)
-                project(stream, c, first + 1)
-
-        def bind(c, t):
-            if t == 0:
-                planes[c] = ring.tile([P, PACK, BLOCK], BF16, name="planes", tag="planes", bufs=3)
-            k_biased = ring.tile([P, BLOCK], F32, name="k_biased", tag="k_biased", bufs=4)
+        def add_bias_k(c, t):
+            if c not in live:
+                return
+            biased[(c, t)] = ring.tile([P, BLOCK], F32, name="biased", tag="biased", bufs=6)
             nc.scalar.activation(
-                out=k_biased[:], in_=projected[("k", c, t)][:], func=IDENTITY,
+                out=biased[(c, t)][:], in_=projected[("k", c, t)][:], func=IDENTITY,
                 bias=bias_k[:, t : t + 1], scale=1.0,
             )
+
+        def bind(c, t):
+            if c not in live:
+                return
+            if t == 0:
+                planes[c] = ring.tile([P, PACK, BLOCK], BF16, name="planes", tag="planes")
             nc.vector.scalar_tensor_tensor(
                 out=planes[c][:, t, :], in0=projected[("v", c, t)][:], scalar=bias_v[:, t : t + 1],
-                in1=k_biased[:], op0=ADD, op1=MULT,
+                in1=biased[(c, t)][:], op0=ADD, op1=MULT,
             )
 
         def regroup(copy, c, first, last):
+            if c not in live:
+                return
+            if ("p", c) not in grouped:
+                grouped[("p", c)] = ring.tile(
+                    [P, BLOCK * PACK], BF16, name="grouped_p", tag="grouped_p", align_bytes=64
+                )
             by_token = grouped[("p", c)][:].rearrange("r (n t) -> r n t", t=PACK)
             copy(
                 out=by_token[:, first:last, :].rearrange("r (m s) t -> r m t s", s=4),
                 in_=planes[c][:, :, first:last].rearrange("r t (m s) -> r m t s", s=4),
             )
 
-        def regroup_by_gpsimd(c, first, last):
+        def regroup_on_gpsimd(c, first, last):
+            if c not in live:
+                return
+            if ("p", c) not in grouped:
+                grouped[("p", c)] = ring.tile(
+                    [P, BLOCK * PACK], BF16, name="grouped_p", tag="grouped_p", align_bytes=64
+                )
             by_token = grouped[("p", c)][:].rearrange("r (n t) -> r n t", t=PACK)
             nc.gpsimd.tensor_scalar(
                 out=by_token[:, first:last, :],
@@ -183,97 +222,113 @@ def tile_learnedbindingmemory_pa_t_kernel(
                 scalar1=1.0, scalar2=0.0, op0=MULT, op1=ADD,
             )
 
-        def quantise_product(c, half):
-            product = ("p", c)
-            first, last = half * 2 * P, (half + 1) * 2 * P
-            if half == 0:
-                grouped[product] = ring.tile(
-                    [P, BLOCK * PACK], BF16, name="grouped_p", tag="grouped_p", align_bytes=64
-                )
-                packed_tiles(product, ring)
-                regroup_by_gpsimd(c, 2 * P, 4 * P)
-                regroup(nc.scalar.copy, c, first, first + P)
-                regroup(nc.scalar.copy, c, first + P, last)
-            nc.vector.quantize_mx(
-                out=codes[product][:, first:last].bitcast(FP8X4),
-                scales=scales[product][:, first:last],
-                in_=grouped[product][:, first * PACK : last * PACK],
-            )
-
         def combine(c, i):
+            if c not in live:
+                return
             tokens = slice(i * P, (i + 1) * P)
-            bank = psum.tile([P, WIDTH], F32, name="combined", tag="combined")
+            bank = psum.tile([P, WIDTH], F32, name="combined", tag=FOR_VECTOR)
             nc.tensor.matmul_mx(
                 out=bank[:],
                 lhsT=codes[("p", c)][:, tokens].bitcast(FP8X4),
                 lhsT_scale=scales[("p", c)][:, tokens],
-                rhs=codes[("wc", 0)][:].bitcast(FP8X4),
-                rhs_scale=scales[("wc", 0)][:],
+                rhs=codes[WC][:].bitcast(FP8X4),
+                rhs_scale=scales[WC][:],
                 start=True,
                 stop=True,
             )
             combined[(c, i)] = bank
 
         def finish(c, i):
+            if c not in live:
+                return
             result = ring.tile([P, WIDTH], F32, name="result", tag="result", bufs=6)
             nc.vector.tensor_tensor(out=result[:], in0=combined[(c, i)][:], in1=bias_c[:], op=ADD)
             nc.sync.dma_start(
-                out=chunk_of(out_rows, c).rearrange(NEIGHBOURS, i=TILES)[:, i, :], in_=result[:]
+                out=out_rows[c * BLOCK : (c + 1) * BLOCK, :].rearrange(NEIGHBOURS, i=TILES)[:, i, :],
+                in_=result[:],
             )
 
         bias_c = fixed.tile([P, WIDTH], F32)
 
         def spread_bias_c():
-            spread = psum.tile([P, WIDTH], F32, name="spread", tag="combined")
+            spread = psum.tile([P, WIDTH], F32, name="spread", tag=FOR_VECTOR)
             nc.tensor.matmul(out=spread[:], lhsT=ones[:], rhs=bias_row[:], start=True, stop=True)
             nc.vector.tensor_copy(out=bias_c[:], in_=spread[:])
 
-        prepare(("wk", 0), fixed, "projected_k", BY_BOTH)
-        prepare(("k", 0), ring, "turned", BY_BOTH)
-        prepare(("wv", 0), fixed, "projected_v", BY_BOTH)
-        prepare(("v", 0), ring, "combined", BY_BOTH)
-        transpose(("k", 1))
-        project_pair(0, 0)
-        gather(("k", 1), BY_SCALAR)
-        transpose(("v", 1))
-
-        live = range(CHUNKS)
-        for a in range(CHUNKS + 2):
-            if a in live:
-                bind(a, 0)
-                bind(a, 1)
-            if a - 2 in live:
-                combine(a - 2, 2)
-                combine(a - 2, 3)
-            if a in live:
-                project_pair(a, 2)
-            if a + 1 in live:
-                quantise(("k", a + 1), ring)
-            if a - 1 in live:
-                quantise_product(a - 1, 0)
-            if a - 2 in live:
-                finish(a - 2, 2)
-                finish(a - 2, 3)
-            if a + 1 in live:
-                gather(("v", a + 1), BY_SCALAR)
-                quantise(("v", a + 1), ring)
-            if a + 2 in live:
-                transpose(("k", a + 2))
-            if a - 1 in live:
-                combine(a - 1, 0)
-                combine(a - 1, 1)
-            if a in live:
-                bind(a, 2)
-                bind(a, 3)
-            if a == 0:
+        for n, (block, half) in enumerate(first_halves):
+            if n == 4:
                 spread_bias_c()
-                prepare(("wc", 0), fixed, "combined", BY_VECTOR, PAIRS)
-            if a + 1 in live:
-                project_pair(a + 1, 0)
-            if a - 1 in live:
-                quantise_product(a - 1, 1)
-                finish(a - 1, 0)
-                finish(a - 1, 1)
-            if a + 2 in live:
-                gather(("k", a + 2), BY_SCALAR)
-                transpose(("v", a + 2))
+            transpose(block, half, FOR_SCALAR if n < 4 else FOR_VECTOR)
+            gather(block, half)
+            if half == 0:
+                packed_tiles(block)
+            quantise_rows(block, half * HALF, (half + 1) * HALF)
+        for t0 in (0, 2):
+            for stream in ("k", "v"):
+                project(stream, 0, t0)
+                project(stream, 0, t0 + 1)
+        transpose(("k", 1), 0)
+        transpose(("k", 1), 1)
+        for t in range(PACK):
+            add_bias_k(0, t)
+            bind(0, t)
+        gather(("k", 1), 0)
+        transpose(("v", 1), 0)
+        transpose(("v", 1), 1)
+        regroup(nc.scalar.copy, 0, 0, HALF)
+        regroup(nc.vector.tensor_copy, 0, HALF, BLOCK)
+        gather(("k", 1), 1)
+        gather(("v", 1), 0)
+        quantise(("k", 1))
+        quantise(("p", 0))
+        gather(("v", 1), 1)
+        quantise(("v", 1))
+        transpose(WC, 0, FOR_VECTOR)
+        transpose(WC, 1, FOR_VECTOR)
+        gather(WC, 0, nc.vector.tensor_copy)
+        gather(WC, 1)
+        quantise(WC)
+        transpose(("k", 2), 0)
+        transpose(("k", 2), 1)
+        gather(("k", 2), 0)
+        transpose(("v", 2), 0)
+        transpose(("v", 2), 1)
+        gather(("k", 2), 1)
+        gather(("v", 2), 0)
+        gather(("v", 2), 1)
+        for t in range(PACK):
+            project("k", 1, t)
+            project("v", 1, t)
+        quantise(("k", 2))
+        quantise(("v", 2))
+
+        for a in range(1, CHUNKS + 1):
+            for t in range(PACK):
+                add_bias_k(a, t)
+                bind(a, t)
+                if t == 1:
+                    transpose(("k", a + 2), 0)
+                    transpose(("k", a + 2), 1)
+                    combine(a - 1, 0)
+                    combine(a - 1, 1)
+            combine(a - 1, 2)
+            combine(a - 1, 3)
+            regroup_on_gpsimd(a, BLOCK - GPSIMD_REGROUPS, BLOCK)
+            gather(("k", a + 2), 0)
+            finish(a - 1, 0)
+            finish(a - 1, 1)
+            transpose(("v", a + 2), 0)
+            transpose(("v", a + 2), 1)
+            regroup(nc.scalar.copy, a, 0, BLOCK - GPSIMD_REGROUPS)
+            gather(("k", a + 2), 1)
+            finish(a - 1, 2)
+            finish(a - 1, 3)
+            gather(("v", a + 2), 0)
+            gather(("v", a + 2), 1)
+            if a in live:
+                quantise(("p", a))
+            for t in range(PACK):
+                project("k", a + 1, t)
+                project("v", a + 1, t)
+            quantise(("k", a + 2))
+            quantise(("v", a + 2))

@@ -21,6 +21,7 @@ TOKENS = 4 * 1024
 CHUNKS = TOKENS // BLOCK
 HALF = BLOCK // 2
 GPSIMD_REGROUPS = 256
+SHARED = (1, 2, 4, 5)
 
 FLOPS = 3 * 2 * TOKENS * WIDTH * WIDTH
 
@@ -48,6 +49,7 @@ def tile_learnedbindingmemory_pa_t_kernel(
         projected = {}
         biased = {}
         planes = {}
+        drained = {}
         combined = {}
 
         NEIGHBOURS = "(r i) d -> r i d"
@@ -243,6 +245,18 @@ def tile_learnedbindingmemory_pa_t_kernel(
                 return
             result = ring.tile([P, WIDTH], F32, name="result", tag="result", bufs=6)
             nc.vector.tensor_tensor(out=result[:], in0=combined[(c, i)][:], in1=bias_c[:], op=ADD)
+            store(c, i, result)
+
+        def drain(c, i):
+            drained[c] = ring.tile([P, WIDTH], F32, name="drained", tag="drained")
+            nc.scalar.copy(out=drained[c][:], in_=combined[(c, i)][:])
+
+        def finish_on_gpsimd(c, i):
+            result = ring.tile([P, WIDTH], F32, name="result_g", tag="result_g")
+            nc.gpsimd.tensor_tensor(out=result[:], in0=drained[c][:], in1=bias_c[:], op=ADD)
+            store(c, i, result)
+
+        def store(c, i, result):
             nc.sync.dma_start(
                 out=out_rows[c * BLOCK : (c + 1) * BLOCK, :].rearrange(NEIGHBOURS, i=TILES)[:, i, :],
                 in_=result[:],
@@ -302,33 +316,57 @@ def tile_learnedbindingmemory_pa_t_kernel(
         quantise(("k", 2))
         quantise(("v", 2))
 
-        for a in range(1, CHUNKS + 1):
-            for t in range(PACK):
-                add_bias_k(a, t)
-                bind(a, t)
-                if t == 1:
-                    transpose(("k", a + 2), 0)
-                    transpose(("k", a + 2), 1)
-                    combine(a - 1, 0)
-                    combine(a - 1, 1)
-            combine(a - 1, 2)
-            combine(a - 1, 3)
-            regroup_on_gpsimd(a, BLOCK - GPSIMD_REGROUPS, BLOCK)
-            gather(("k", a + 2), 0)
-            finish(a - 1, 0)
-            finish(a - 1, 1)
-            transpose(("v", a + 2), 0)
-            transpose(("v", a + 2), 1)
-            regroup(nc.scalar.copy, a, 0, BLOCK - GPSIMD_REGROUPS)
-            gather(("k", a + 2), 1)
-            finish(a - 1, 2)
-            finish(a - 1, 3)
-            gather(("v", a + 2), 0)
-            gather(("v", a + 2), 1)
-            if a in live:
-                quantise(("p", a))
-            for t in range(PACK):
-                project("k", a + 1, t)
-                project("v", a + 1, t)
-            quantise(("k", a + 2))
-            quantise(("v", a + 2))
+        for b in range(1, CHUNKS + 2):
+            started = b == 1
+            if b > 2:
+                quantise(("v", b))
+            if not started:
+                project("v", b, 0)
+                transpose(("v", b + 1), 0)
+            if b - 3 in SHARED:
+                finish_on_gpsimd(b - 3, 3)
+            if not started:
+                regroup_on_gpsimd(b - 1, BLOCK - GPSIMD_REGROUPS, BLOCK)
+            finish(b - 2, 0)
+            if not started:
+                gather(("k", b + 1), 1)
+            finish(b - 2, 1)
+            if not started:
+                project("k", b, 2)
+            combine(b - 2, 3)
+            add_bias_k(b, 0)
+            finish(b - 2, 2)
+            if not started:
+                regroup(nc.scalar.copy, b - 1, 0, BLOCK - GPSIMD_REGROUPS)
+                project("k", b, 3)
+                project("v", b, 1)
+                project("v", b, 2)
+                project("v", b, 3)
+            bind(b, 0)
+            add_bias_k(b, 1)
+            if not started:
+                transpose(("v", b + 1), 1)
+                quantise(("k", b + 1))
+            add_bias_k(b, 2)
+            transpose(("k", b + 2), 0)
+            transpose(("k", b + 2), 1)
+            if not started and b - 1 in live:
+                quantise(("p", b - 1))
+            if b - 2 in SHARED:
+                drain(b - 2, 3)
+            else:
+                finish(b - 2, 3)
+            if not started:
+                gather(("v", b + 1), 0)
+            bind(b, 1)
+            add_bias_k(b, 3)
+            combine(b - 1, 0)
+            project("k", b + 1, 0)
+            bind(b, 2)
+            combine(b - 1, 1)
+            project("k", b + 1, 1)
+            if not started:
+                gather(("v", b + 1), 1)
+            bind(b, 3)
+            combine(b - 1, 2)
+            gather(("k", b + 2), 0)

@@ -92,12 +92,15 @@ def tile_learnedbindingmemory_pa_t_kernel(
         ones = fixed.tile([P, P], BF16)
         nc.vector.memset(bias_row[:], 0.0)
         nc.vector.memset(ones[:], 1.0)
-        nc.scalar.dma_start(out=bias_k16[:], in_=bbk.rearrange("(r t) -> r t", t=PACK))
-        nc.scalar.dma_start(out=bias_v16[:], in_=bbv.rearrange("(r t) -> r t", t=PACK))
-        nc.scalar.dma_start(out=bias_row[0:1, :], in_=bbc.unsqueeze(0))
+        first_activation = fixed.tile([P, 1], F32)
+        nc.scalar.activation(out=first_activation[:], in_=ones[:, 0:1], func=IDENTITY)
 
-        for block, half in first_halves:
+        for n, (block, half) in enumerate(first_halves):
+            if n == 6:
+                nc.sync.dma_start(out=bias_k16[:], in_=bbk.rearrange("(r t) -> r t", t=PACK))
+                nc.sync.dma_start(out=bias_v16[:], in_=bbv.rearrange("(r t) -> r t", t=PACK))
             load_half(block, half)
+        nc.sync.dma_start(out=bias_row[0:1, :], in_=bbc.unsqueeze(0))
         load(("k", 1))
         load(("v", 1))
         load(WC)
@@ -107,8 +110,6 @@ def tile_learnedbindingmemory_pa_t_kernel(
 
         bias_k = fixed.tile([P, PACK], F32)
         bias_v = fixed.tile([P, PACK], F32)
-        nc.scalar.activation(out=bias_k[:], in_=bias_k16[:], func=IDENTITY)
-        nc.scalar.activation(out=bias_v[:], in_=bias_v16[:], func=IDENTITY)
 
         FOR_SCALAR, FOR_VECTOR = "for_scalar", "for_vector"
 
@@ -247,6 +248,14 @@ def tile_learnedbindingmemory_pa_t_kernel(
             nc.vector.tensor_tensor(out=result[:], in0=combined[(c, i)][:], in1=bias_c[:], op=ADD)
             store(c, i, result)
 
+        def finish_columns(c, i, first, last):
+            result = ring.tile([P, last - first], F32, name="result_part", tag="result_part")
+            nc.vector.tensor_tensor(
+                out=result[:], in0=combined[(c, i)][:, first:last], in1=bias_c[:, first:last], op=ADD
+            )
+            rows = out_rows[c * BLOCK : (c + 1) * BLOCK, :].rearrange(NEIGHBOURS, i=TILES)
+            nc.sync.dma_start(out=rows[:, i, first:last], in_=result[:])
+
         def drain(c, i):
             drained[c] = ring.tile([P, WIDTH], F32, name="drained", tag="drained")
             nc.scalar.copy(out=drained[c][:], in_=combined[(c, i)][:])
@@ -270,13 +279,14 @@ def tile_learnedbindingmemory_pa_t_kernel(
             nc.vector.tensor_copy(out=bias_c[:], in_=spread[:])
 
         for n, (block, half) in enumerate(first_halves):
-            if n == 4:
-                spread_bias_c()
             transpose(block, half, FOR_SCALAR if n < 4 else FOR_VECTOR)
             gather(block, half)
             if half == 0:
                 packed_tiles(block)
             quantise_rows(block, half * HALF, (half + 1) * HALF)
+            if n == 5:
+                nc.vector.tensor_copy(out=bias_k[:], in_=bias_k16[:])
+                nc.vector.tensor_copy(out=bias_v[:], in_=bias_v16[:])
         for t0 in (0, 2):
             for stream in ("k", "v"):
                 project(stream, 0, t0)
@@ -291,6 +301,7 @@ def tile_learnedbindingmemory_pa_t_kernel(
         transpose(("v", 1), 1)
         regroup(nc.scalar.copy, 0, 0, HALF)
         regroup(nc.vector.tensor_copy, 0, HALF, BLOCK)
+        spread_bias_c()
         gather(("k", 1), 1)
         gather(("v", 1), 0)
         quantise(("k", 1))
@@ -354,6 +365,9 @@ def tile_learnedbindingmemory_pa_t_kernel(
                 quantise(("p", b - 1))
             if b - 2 in SHARED:
                 drain(b - 2, 3)
+            elif b - 2 == CHUNKS - 1:
+                finish_columns(b - 2, 3, 0, WIDTH // 2)
+                finish_columns(b - 2, 3, WIDTH // 2, WIDTH)
             else:
                 finish(b - 2, 3)
             if not started:

@@ -333,34 +333,32 @@ def tile_learnedbindingmemory_pa_t_kernel(
                 quantise(("v", b))
             if not started:
                 project("v", b, 0)
-                transpose(("v", b + 1), 0)
+                project("k", b, 2)
             if b - 3 in SHARED:
                 finish_on_gpsimd(b - 3, 3)
             if not started:
                 regroup_on_gpsimd(b - 1, BLOCK - GPSIMD_REGROUPS, BLOCK)
             finish(b - 2, 0)
-            if not started:
-                gather(("k", b + 1), 1)
             finish(b - 2, 1)
-            if not started:
-                project("k", b, 2)
             combine(b - 2, 3)
-            add_bias_k(b, 0)
-            finish(b - 2, 2)
             if not started:
-                regroup(nc.scalar.copy, b - 1, 0, BLOCK - GPSIMD_REGROUPS)
-                project("k", b, 3)
                 project("v", b, 1)
+                transpose(("v", b + 1), 0)
+                transpose(("v", b + 1), 1)
+                project("k", b, 3)
                 project("v", b, 2)
                 project("v", b, 3)
-            bind(b, 0)
-            add_bias_k(b, 1)
-            if not started:
-                transpose(("v", b + 1), 1)
-                quantise(("k", b + 1))
-            add_bias_k(b, 2)
             transpose(("k", b + 2), 0)
             transpose(("k", b + 2), 1)
+            finish(b - 2, 2)
+            add_bias_k(b, 0)
+            if not started:
+                regroup(nc.scalar.copy, b - 1, 0, BLOCK - GPSIMD_REGROUPS)
+            add_bias_k(b, 1)
+            bind(b, 0)
+            if not started:
+                quantise(("k", b + 1))
+            add_bias_k(b, 2)
             if not started and b - 1 in live:
                 quantise(("p", b - 1))
             if b - 2 in SHARED:
@@ -372,15 +370,16 @@ def tile_learnedbindingmemory_pa_t_kernel(
                 finish(b - 2, 3)
             if not started:
                 gather(("v", b + 1), 0)
-            bind(b, 1)
             add_bias_k(b, 3)
-            combine(b - 1, 0)
-            project("k", b + 1, 0)
-            bind(b, 2)
-            combine(b - 1, 1)
-            project("k", b + 1, 1)
             if not started:
                 gather(("v", b + 1), 1)
-            bind(b, 3)
+            combine(b - 1, 0)
+            project("k", b + 1, 0)
+            bind(b, 1)
+            combine(b - 1, 1)
+            project("k", b + 1, 1)
+            bind(b, 2)
             combine(b - 1, 2)
+            bind(b, 3)
             gather(("k", b + 2), 0)
+            gather(("k", b + 2), 1)

@@ -20,8 +20,8 @@ TILES = BLOCK // P
 TOKENS = 4 * 1024
 CHUNKS = TOKENS // BLOCK
 HALF = BLOCK // 2
-GPSIMD_REGROUPS = 256
-SHARED = (1, 2, 4, 5)
+GPSIMD_REGROUPS = 320
+SHARED = (1, 2, 3, 4, 5)
 
 FLOPS = 3 * 2 * TOKENS * WIDTH * WIDTH
 
@@ -50,6 +50,8 @@ def tile_learnedbindingmemory_pa_t_kernel(
         biased = {}
         planes = {}
         drained = {}
+        partner = {("k", c): ("p", c - 2) for c in range(3, CHUNKS)}
+        paired = {}
         combined = {}
 
         NEIGHBOURS = "(r i) d -> r i d"
@@ -67,8 +69,8 @@ def tile_learnedbindingmemory_pa_t_kernel(
         def load(block):
             tile = fixed.tile([P, TILES * WIDTH], BF16, name="raw_%s_%s" % block)
             nc.sync.dma_start(out=tile[:].rearrange("r (i d) -> r i d", i=TILES), in_=rows_of(block))
-            for half in range(2):
-                raw[(block, half)] = tile[:, half * 2 * WIDTH : (half + 1) * 2 * WIDTH]
+            for i in range(TILES):
+                raw[(block, i)] = tile[:, i * WIDTH : (i + 1) * WIDTH]
 
         def load_half(block, half):
             tile = fixed.tile([P, 2 * WIDTH], BF16, name="raw_%s_%s_half%s" % (block + (half,)))
@@ -76,7 +78,13 @@ def tile_learnedbindingmemory_pa_t_kernel(
                 out=tile[:].rearrange("r (j d) -> r j d", j=2),
                 in_=rows_of(block)[:, 2 * half : 2 * half + 2, :],
             )
-            raw[(block, half)] = tile[:]
+            for j in range(2):
+                raw[(block, 2 * half + j)] = tile[:, j * WIDTH : (j + 1) * WIDTH]
+
+        def load_row_tile(block, i):
+            tile = fixed.tile([P, WIDTH], BF16, name="raw_%s_%s_tile%s" % (block + (i,)))
+            nc.sync.dma_start(out=tile[:], in_=rows_of(block)[:, i, :])
+            raw[(block, i)] = tile[:]
 
         WK, WV, WC = ("wk", 0), ("wv", 0), ("wc", 0)
         first_halves = [
@@ -99,7 +107,11 @@ def tile_learnedbindingmemory_pa_t_kernel(
             if n == 6:
                 nc.sync.dma_start(out=bias_k16[:], in_=bbk.rearrange("(r t) -> r t", t=PACK))
                 nc.sync.dma_start(out=bias_v16[:], in_=bbv.rearrange("(r t) -> r t", t=PACK))
-            load_half(block, half)
+            if n == 0:
+                load_row_tile(block, 0)
+                load_row_tile(block, 1)
+            else:
+                load_half(block, half)
         nc.sync.dma_start(out=bias_row[0:1, :], in_=bbc.unsqueeze(0))
         load(("k", 1))
         load(("v", 1))
@@ -119,17 +131,24 @@ def tile_learnedbindingmemory_pa_t_kernel(
         def transpose(block, half, emptied=FOR_SCALAR):
             if not exists(block):
                 return
-            words = raw[(block, half)].bitcast(F32).rearrange("r (j q u) -> r j u q", j=2, u=2)
             bank = psum.tile([P, 2, 2, P], F32, name="turned", tag=emptied)
             for j in range(2):
+                words = raw[(block, 2 * half + j)].bitcast(F32).rearrange("r (q u) -> r u q", u=2)
                 for u in range(2):
-                    nc.tensor.transpose(bank[:, j, u, :], words[:, j, u, :], identity[:])
+                    nc.tensor.transpose(bank[:, j, u, :], words[:, u, :], identity[:])
             turned[(block, half)] = bank
 
         def gather(block, half, copy=nc.scalar.copy):
             if not exists(block):
                 return
-            if half == 0:
+            if half == 0 and block in partner:
+                pair = ring.tile(
+                    [P, 2 * BLOCK * PACK], BF16, name="grouped_pair", tag="grouped_pair", align_bytes=64
+                )
+                grouped[block] = pair[:, 0 : BLOCK * PACK]
+                grouped[partner[block]] = pair[:, BLOCK * PACK : 2 * BLOCK * PACK]
+                paired[block] = pair
+            elif half == 0:
                 grouped[block] = ring.tile(
                     [P, BLOCK * PACK], BF16, name="grouped", tag="grouped", bufs=6, align_bytes=64
                 )
@@ -160,6 +179,16 @@ def tile_learnedbindingmemory_pa_t_kernel(
             if exists(block):
                 packed_tiles(block)
                 quantise_rows(block, 0, BLOCK)
+
+        def quantise_pair(block):
+            both = ring.tile([P, 2 * BLOCK], U32, name="codes_pair", tag="codes_pair", align_bytes=64)
+            plane = ring.tile([P, 2 * BLOCK], U8, name="scales_pair", tag="scales_pair", align_bytes=64)
+            nc.vector.quantize_mx(
+                out=both[:].bitcast(FP8X4), scales=plane[:], in_=paired[block][:]
+            )
+            for n, member in enumerate((block, partner[block])):
+                codes[member] = both[:, n * BLOCK : (n + 1) * BLOCK]
+                scales[member] = plane[:, n * BLOCK : (n + 1) * BLOCK]
 
         def project(stream, c, t):
             if c not in live:
@@ -327,7 +356,7 @@ def tile_learnedbindingmemory_pa_t_kernel(
         quantise(("k", 2))
         quantise(("v", 2))
 
-        for b in range(1, CHUNKS + 2):
+        for b in range(1, CHUNKS):
             started = b == 1
             if b > 2:
                 quantise(("v", b))
@@ -356,16 +385,13 @@ def tile_learnedbindingmemory_pa_t_kernel(
                 regroup(nc.scalar.copy, b - 1, 0, BLOCK - GPSIMD_REGROUPS)
             add_bias_k(b, 1)
             bind(b, 0)
-            if not started:
-                quantise(("k", b + 1))
-            add_bias_k(b, 2)
-            if not started and b - 1 in live:
+            if not started and ("k", b + 1) in partner:
+                quantise_pair(("k", b + 1))
+            elif not started and b - 1 in live:
                 quantise(("p", b - 1))
+            add_bias_k(b, 2)
             if b - 2 in SHARED:
                 drain(b - 2, 3)
-            elif b - 2 == CHUNKS - 1:
-                finish_columns(b - 2, 3, 0, WIDTH // 2)
-                finish_columns(b - 2, 3, WIDTH // 2, WIDTH)
             else:
                 finish(b - 2, 3)
             if not started:
@@ -383,3 +409,26 @@ def tile_learnedbindingmemory_pa_t_kernel(
             bind(b, 3)
             gather(("k", b + 2), 0)
             gather(("k", b + 2), 1)
+
+        last = CHUNKS - 1
+        if last - 2 in SHARED:
+            finish_on_gpsimd(last - 2, 3)
+        regroup_on_gpsimd(last, P, HALF)
+        regroup(nc.scalar.copy, last, 0, P)
+        finish(last - 1, 0)
+        combine(last - 1, 3)
+        finish(last - 1, 1)
+        packed_tiles(("p", last))
+        quantise_rows(("p", last), 0, HALF)
+        combine(last, 0)
+        combine(last, 1)
+        regroup(nc.scalar.copy, last, HALF, BLOCK)
+        finish(last - 1, 2)
+        quantise_rows(("p", last), HALF, BLOCK)
+        finish(last - 1, 3)
+        combine(last, 2)
+        combine(last, 3)
+        for i in range(TILES - 1):
+            finish(last, i)
+        finish_columns(last, TILES - 1, 0, WIDTH // 2)
+        finish_columns(last, TILES - 1, WIDTH // 2, WIDTH)

@@ -20,7 +20,7 @@ TILES = BLOCK // P
 TOKENS = 4 * 1024
 CHUNKS = TOKENS // BLOCK
 HALF = BLOCK // 2
-GPSIMD_REGROUPS = 320
+GPSIMD_REGROUPS = 352
 SHARED = (1, 2, 3, 4, 5)
 
 FLOPS = 3 * 2 * TOKENS * WIDTH * WIDTH

@@ -42,6 +42,7 @@ def tile_learnedbindingmemory_pa_t_kernel(
 
         live = range(CHUNKS)
         raw = {}
+        split = set()
         turned = {}
         grouped = {}
         codes = {}
@@ -133,7 +134,8 @@ def tile_learnedbindingmemory_pa_t_kernel(
                 return
             bank = psum.tile([P, 2, 2, P], F32, name="turned", tag=emptied)
             for j in range(2):
-                words = raw[(block, 2 * half + j)].bitcast(F32).rearrange("r (q u) -> r u q", u=2)
+                order = "r (u q) -> r u q" if block in split else "r (q u) -> r u q"
+                words = raw[(block, 2 * half + j)].bitcast(F32).rearrange(order, u=2)
                 for u in range(2):
                     nc.tensor.transpose(bank[:, j, u, :], words[:, u, :], identity[:])
             turned[(block, half)] = bank
@@ -189,6 +191,17 @@ def tile_learnedbindingmemory_pa_t_kernel(
             for n, member in enumerate((block, partner[block])):
                 codes[member] = both[:, n * BLOCK : (n + 1) * BLOCK]
                 scales[member] = plane[:, n * BLOCK : (n + 1) * BLOCK]
+
+        def split_words_on_gpsimd(block):
+            for i in range(TILES):
+                words = fixed.tile([P, WIDTH], BF16, name="split_%s_%s_%s" % (block + (i,)))
+                nc.gpsimd.tensor_scalar(
+                    out=words[:].rearrange("r (u q e) -> r u q e", u=2, e=2),
+                    in0=raw[(block, i)].rearrange("r (q u e) -> r u q e", u=2, e=2),
+                    scalar1=1.0, scalar2=0.0, op0=MULT, op1=ADD,
+                )
+                raw[(block, i)] = words[:]
+            split.add(block)
 
         def project(stream, c, t):
             if c not in live:
@@ -286,7 +299,7 @@ def tile_learnedbindingmemory_pa_t_kernel(
             nc.sync.dma_start(out=rows[:, i, first:last], in_=result[:])
 
         def drain(c, i):
-            drained[c] = ring.tile([P, WIDTH], F32, name="drained", tag="drained")
+            drained[c] = ring.tile([P, WIDTH], F32, name="drained", tag="drained", bufs=2)
             nc.scalar.copy(out=drained[c][:], in_=combined[(c, i)][:])
 
         def finish_on_gpsimd(c, i):
@@ -328,6 +341,7 @@ def tile_learnedbindingmemory_pa_t_kernel(
         gather(("k", 1), 0)
         transpose(("v", 1), 0)
         transpose(("v", 1), 1)
+        split_words_on_gpsimd(WC)
         regroup(nc.scalar.copy, 0, 0, HALF)
         regroup(nc.vector.tensor_copy, 0, HALF, BLOCK)
         spread_bias_c()

from contextlib import ExitStack

import concourse.mybir as mybir
from concourse.masks import make_identity

F32 = mybir.dt.float32
BF16 = mybir.dt.bfloat16
U32 = mybir.dt.uint32
U8 = mybir.dt.uint8
FP8X4 = mybir.dt.float8_e4m3fn_x4
ADD = mybir.AluOpType.add
MULT = mybir.AluOpType.mult
IDENTITY = mybir.ActivationFunctionType.Identity

P = 128
PACK = 4
WIDTH = P * PACK
BLOCK = 512
TILES = BLOCK // P
TOKENS = 4 * 1024
CHUNKS = TOKENS // BLOCK
HALF = BLOCK // 2
GPSIMD_REGROUPS = 352
SHARED = (1, 2, 3, 4, 5)

FLOPS = 3 * 2 * TOKENS * WIDTH * WIDTH


def tile_learnedbindingmemory_pa_t_kernel(
    tc, keys, values, Wbk, bbk, Wbv, bbv, Wbc, bbc, out
):
    nc = tc.nc
    key_rows = keys.flatten_outer_dims()
    value_rows = values.flatten_outer_dims()
    out_rows = out.flatten_outer_dims()

    with ExitStack() as ctx:
        ctx.enter_context(tc.manual_schedule())
        fixed = ctx.enter_context(tc.tile_pool(name="fixed", bufs=1))
        ring = ctx.enter_context(tc.tile_pool(name="ring", bufs=3))
        psum = ctx.enter_context(tc.psum_pool(name="psum", bufs=4))

        live = range(CHUNKS)
        raw = {}
        split = set()
        turned = {}
        grouped = {}
        codes = {}
        scales = {}
        projected = {}
        biased = {}
        planes = {}
        drained = {}
        partner = {("k", c): ("p", c - 2) for c in range(3, CHUNKS)}
        paired = {}
        combined = {}

        NEIGHBOURS = "(r i) d -> r i d"
        STRIPES = "(i r) d -> r i d"

        def rows_of(block):
            kind, c = block
            if kind in ("k", "v"):
                rows = key_rows if kind == "k" else value_rows
                return rows[c * BLOCK : (c + 1) * BLOCK, :].rearrange(NEIGHBOURS, i=TILES)
            if kind == "wc":
                return Wbc.rearrange(STRIPES, i=TILES)
            return (Wbk if kind == "wk" else Wbv).rearrange(NEIGHBOURS, i=TILES)

        def load(block):
            tile = fixed.tile([P, TILES * WIDTH], BF16, name="raw_%s_%s" % block)
            nc.sync.dma_start(out=tile[:].rearrange("r (i d) -> r i d", i=TILES), in_=rows_of(block))
            for i in range(TILES):
                raw[(block, i)] = tile[:, i * WIDTH : (i + 1) * WIDTH]

        def load_half(block, half):
            tile = fixed.tile([P, 2 * WIDTH], BF16, name="raw_%s_%s_half%s" % (block + (half,)))
            nc.sync.dma_start(
                out=tile[:].rearrange("r (j d) -> r j d", j=2),
                in_=rows_of(block)[:, 2 * half : 2 * half + 2, :],
            )
            for j in range(2):
                raw[(block, 2 * half + j)] = tile[:, j * WIDTH : (j + 1) * WIDTH]

        def load_row_tile(block, i):
            tile = fixed.tile([P, WIDTH], BF16, name="raw_%s_%s_tile%s" % (block + (i,)))
            nc.sync.dma_start(out=tile[:], in_=rows_of(block)[:, i, :])
            raw[(block, i)] = tile[:]

        WK, WV, WC = ("wk", 0), ("wv", 0), ("wc", 0)
        first_halves = [
            (WK, 0), (("k", 0), 0), (("k", 0), 1), (WV, 0), (("v", 0), 0), (("v", 0), 1),
            (WK, 1), (WV, 1),
        ]

        identity = fixed.tile([P, P], F32)
        make_identity(nc, identity[:])
        bias_k16 = fixed.tile([P, PACK], BF16)
        bias_v16 = fixed.tile([P, PACK], BF16)
        bias_row = fixed.tile([P, WIDTH], BF16)
        ones = fixed.tile([P, P], BF16)
        nc.vector.memset(bias_row[:], 0.0)
        nc.vector.memset(ones[:], 1.0)
        first_activation = fixed.tile([P, 1], F32)
        nc.scalar.activation(out=first_activation[:], in_=ones[:, 0:1], func=IDENTITY)

        for n, (block, half) in enumerate(first_halves):
            if n == 6:
                nc.sync.dma_start(out=bias_k16[:], in_=bbk.rearrange("(r t) -> r t", t=PACK))
                nc.sync.dma_start(out=bias_v16[:], in_=bbv.rearrange("(r t) -> r t", t=PACK))
            if n == 0:
                load_row_tile(block, 0)
                load_row_tile(block, 1)
            else:
                load_half(block, half)
        nc.sync.dma_start(out=bias_row[0:1, :], in_=bbc.unsqueeze(0))
        load(("k", 1))
        load(("v", 1))
        load(WC)
        for c in range(2, CHUNKS):
            load(("k", c))
            load(("v", c))

        bias_k = fixed.tile([P, PACK], F32)
        bias_v = fixed.tile([P, PACK], F32)

        FOR_SCALAR, FOR_VECTOR = "for_scalar", "for_vector"

        def exists(block):
            return block[0] not in ("k", "v") or block[1] in live

        def transpose(block, half, emptied=FOR_SCALAR):
            if not exists(block):
                return
            bank = psum.tile([P, 2, 2, P], F32, name="turned", tag=emptied)
            for j in range(2):
                order = "r (u q) -> r u q" if block in split else "r (q u) -> r u q"
                words = raw[(block, 2 * half + j)].bitcast(F32).rearrange(order, u=2)
                for u in range(2):
                    nc.tensor.transpose(bank[:, j, u, :], words[:, u, :], identity[:])
            turned[(block, half)] = bank

        def gather(block, half, copy=nc.scalar.copy):
            if not exists(block):
                return
            if half == 0 and block in partner:
                pair = ring.tile(
                    [P, 2 * BLOCK * PACK], BF16, name="grouped_pair", tag="grouped_pair", align_bytes=64
                )
                grouped[block] = pair[:, 0 : BLOCK * PACK]
                grouped[partner[block]] = pair[:, BLOCK * PACK : 2 * BLOCK * PACK]
                paired[block] = pair
            elif half == 0:
                grouped[block] = ring.tile(
                    [P, BLOCK * PACK], BF16, name="grouped", tag="grouped", bufs=6, align_bytes=64
                )
            pairs = grouped[block][:].bitcast(F32).rearrange("q (i n u) -> q i n u", i=TILES, u=2)
            copy(
                out=pairs[:, 2 * half : 2 * half + 2],
                in_=turned[(block, half)][:].rearrange("q j u n -> q j n u"),
            )

        def packed_tiles(block):
            pool = fixed if block in (WK, WV, WC) else ring
            kind = block[0]
            codes[block] = pool.tile(
                [P, BLOCK], U32, name="codes_%s_%s" % block, tag="codes_%s" % kind, align_bytes=64
            )
            scales[block] = pool.tile(
                [P, BLOCK], U8, name="scales_%s_%s" % block, tag="scales_%s" % kind, align_bytes=64
            )

        def quantise_rows(block, first, last):
            nc.vector.quantize_mx(
                out=codes[block][:, first:last].bitcast(FP8X4),
                scales=scales[block][:, first:last],
                in_=grouped[block][:, first * PACK : last * PACK],
            )

        def quantise(block):
            if exists(block):
                packed_tiles(block)
                quantise_rows(block, 0, BLOCK)

        def quantise_pair(block):
            both = ring.tile([P, 2 * BLOCK], U32, name="codes_pair", tag="codes_pair", align_bytes=64)
            plane = ring.tile([P, 2 * BLOCK], U8, name="scales_pair", tag="scales_pair", align_bytes=64)
            nc.vector.quantize_mx(
                out=both[:].bitcast(FP8X4), scales=plane[:], in_=paired[block][:]
            )
            for n, member in enumerate((block, partner[block])):
                codes[member] = both[:, n * BLOCK : (n + 1) * BLOCK]
                scales[member] = plane[:, n * BLOCK : (n + 1) * BLOCK]

        def split_words_on_gpsimd(block):
            for i in range(TILES):
                words = fixed.tile([P, WIDTH], BF16, name="split_%s_%s_%s" % (block + (i,)))
                nc.gpsimd.tensor_scalar(
                    out=words[:].rearrange("r (u q e) -> r u q e", u=2, e=2),
                    in0=raw[(block, i)].rearrange("r (q u e) -> r u q e", u=2, e=2),
                    scalar1=1.0, scalar2=0.0, op0=MULT, op1=ADD,
                )
                raw[(block, i)] = words[:]
            split.add(block)

        def project(stream, c, t):
            if c not in live:
                return
            weight = WK if stream == "k" else WV
            features = slice(t * P, (t + 1) * P)
            emptied = FOR_SCALAR if stream == "k" else FOR_VECTOR
            bank = psum.tile([P, BLOCK], F32, name="projected", tag=emptied)
            nc.tensor.matmul_mx(
                out=bank[:],
                lhsT=codes[weight][:, features].bitcast(FP8X4),
                lhsT_scale=scales[weight][:, features],
                rhs=codes[(stream, c)][:].bitcast(FP8X4),
                rhs_scale=scales[(stream, c)][:],
                start=True,
                stop=True,
            )
            projected[(stream, c, t)] = bank

        def add_bias_k(c, t):
            if c not in live:
                return
            biased[(c, t)] = ring.tile([P, BLOCK], F32, name="biased", tag="biased", bufs=6)
            nc.scalar.activation(
                out=biased[(c, t)][:], in_=projected[("k", c, t)][:], func=IDENTITY,
                bias=bias_k[:, t : t + 1], scale=1.0,
            )

        def bind(c, t):
            if c not in live:
                return
            if t == 0:
                planes[c] = ring.tile([P, PACK, BLOCK], BF16, name="planes", tag="planes")
            nc.vector.scalar_tensor_tensor(
                out=planes[c][:, t, :], in0=projected[("v", c, t)][:], scalar=bias_v[:, t : t + 1],
                in1=biased[(c, t)][:], op0=ADD, op1=MULT,
            )

        def regroup(copy, c, first, last):
            if c not in live:
                return
            if ("p", c) not in grouped:
                grouped[("p", c)] = ring.tile(
                    [P, BLOCK * PACK], BF16, name="grouped_p", tag="grouped_p", align_bytes=64
                )
            by_token = grouped[("p", c)][:].rearrange("r (n t) -> r n t", t=PACK)
            copy(
                out=by_token[:, first:last, :].rearrange("r (m s) t -> r m t s", s=4),
                in_=planes[c][:, :, first:last].rearrange("r t (m s) -> r m t s", s=4),
            )

        def regroup_on_gpsimd(c, first, last):
            if c not in live:
                return
            if ("p", c) not in grouped:
                grouped[("p", c)] = ring.tile(
                    [P, BLOCK * PACK], BF16, name="grouped_p", tag="grouped_p", align_bytes=64
                )
            by_token = grouped[("p", c)][:].rearrange("r (n t) -> r n t", t=PACK)
            nc.gpsimd.tensor_scalar(
                out=by_token[:, first:last, :],
                in0=planes[c][:, :, first:last].rearrange("r t n -> r n t"),
                scalar1=1.0, scalar2=0.0, op0=MULT, op1=ADD,
            )

        def combine(c, i):
            if c not in live:
                return
            tokens = slice(i * P, (i + 1) * P)
            bank = psum.tile([P, WIDTH], F32, name="combined", tag=FOR_VECTOR)
            nc.tensor.matmul_mx(
                out=bank[:],
                lhsT=codes[("p", c)][:, tokens].bitcast(FP8X4),
                lhsT_scale=scales[("p", c)][:, tokens],
                rhs=codes[WC][:].bitcast(FP8X4),
                rhs_scale=scales[WC][:],
                start=True,
                stop=True,
            )
            combined[(c, i)] = bank

        def finish(c, i):
            if c not in live:
                return
            result = ring.tile([P, WIDTH], F32, name="result", tag="result", bufs=6)
            nc.vector.tensor_tensor(out=result[:], in0=combined[(c, i)][:], in1=bias_c[:], op=ADD)
            store(c, i, result)

        def finish_columns(c, i, first, last):
            result = ring.tile([P, last - first], F32, name="result_part", tag="result_part")
            nc.vector.tensor_tensor(
                out=result[:], in0=combined[(c, i)][:, first:last], in1=bias_c[:, first:last], op=ADD
            )
            rows = out_rows[c * BLOCK : (c + 1) * BLOCK, :].rearrange(NEIGHBOURS, i=TILES)
            nc.sync.dma_start(out=rows[:, i, first:last], in_=result[:])

        def drain(c, i):
            drained[c] = ring.tile([P, WIDTH], F32, name="drained", tag="drained", bufs=2)
            nc.scalar.copy(out=drained[c][:], in_=combined[(c, i)][:])

        def finish_on_gpsimd(c, i):
            result = ring.tile([P, WIDTH], F32, name="result_g", tag="result_g")
            nc.gpsimd.tensor_tensor(out=result[:], in0=drained[c][:], in1=bias_c[:], op=ADD)
            store(c, i, result)

        def store(c, i, result):
            nc.sync.dma_start(
                out=out_rows[c * BLOCK : (c + 1) * BLOCK, :].rearrange(NEIGHBOURS, i=TILES)[:, i, :],
                in_=result[:],
            )

        bias_c = fixed.tile([P, WIDTH], F32)

        def spread_bias_c():
            spread = psum.tile([P, WIDTH], F32, name="spread", tag=FOR_VECTOR)
            nc.tensor.matmul(out=spread[:], lhsT=ones[:], rhs=bias_row[:], start=True, stop=True)
            nc.vector.tensor_copy(out=bias_c[:], in_=spread[:])

        for n, (block, half) in enumerate(first_halves):
            transpose(block, half, FOR_SCALAR if n < 4 else FOR_VECTOR)
            gather(block, half)
            if half == 0:
                packed_tiles(block)
            quantise_rows(block, half * HALF, (half + 1) * HALF)
            if n == 5:
                nc.vector.tensor_copy(out=bias_k[:], in_=bias_k16[:])
                nc.vector.tensor_copy(out=bias_v[:], in_=bias_v16[:])
        for t0 in (0, 2):
            for stream in ("k", "v"):
                project(stream, 0, t0)
                project(stream, 0, t0 + 1)
        transpose(("k", 1), 0)
        transpose(("k", 1), 1)
        for t in range(PACK):
            add_bias_k(0, t)
            bind(0, t)
        gather(("k", 1), 0)
        transpose(("v", 1), 0)
        transpose(("v", 1), 1)
        split_words_on_gpsimd(WC)
        regroup(nc.scalar.copy, 0, 0, HALF)
        regroup(nc.vector.tensor_copy, 0, HALF, BLOCK)
        spread_bias_c()
        gather(("k", 1), 1)
        gather(("v", 1), 0)
        quantise(("k", 1))
        quantise(("p", 0))
        gather(("v", 1), 1)
        quantise(("v", 1))
        transpose(WC, 0, FOR_VECTOR)
        transpose(WC, 1, FOR_VECTOR)
        gather(WC, 0, nc.vector.tensor_copy)
        gather(WC, 1)
        quantise(WC)
        transpose(("k", 2), 0)
        transpose(("k", 2), 1)
        gather(("k", 2), 0)
        transpose(("v", 2), 0)
        transpose(("v", 2), 1)
        gather(("k", 2), 1)
        gather(("v", 2), 0)
        gather(("v", 2), 1)
        for t in range(PACK):
            project("k", 1, t)
            project("v", 1, t)
        quantise(("k", 2))
        quantise(("v", 2))

        for b in range(1, CHUNKS):
            started = b == 1
            if b > 2:
                quantise(("v", b))
            if not started:
                project("v", b, 0)
                project("k", b, 2)
            if b - 3 in SHARED:
                finish_on_gpsimd(b - 3, 3)
            if not started:
                regroup_on_gpsimd(b - 1, BLOCK - GPSIMD_REGROUPS, BLOCK)
            finish(b - 2, 0)
            finish(b - 2, 1)
            combine(b - 2, 3)
            if not started:
                project("v", b, 1)
                transpose(("v", b + 1), 0)
                transpose(("v", b + 1), 1)
                project("k", b, 3)
                project("v", b, 2)
                project("v", b, 3)
            transpose(("k", b + 2), 0)
            transpose(("k", b + 2), 1)
            finish(b - 2, 2)
            add_bias_k(b, 0)
            if not started:
                regroup(nc.scalar.copy, b - 1, 0, BLOCK - GPSIMD_REGROUPS)
            add_bias_k(b, 1)
            bind(b, 0)
            if not started and ("k", b + 1) in partner:
                quantise_pair(("k", b + 1))
            elif not started and b - 1 in live:
                quantise(("p", b - 1))
            add_bias_k(b, 2)
            if b - 2 in SHARED:
                drain(b - 2, 3)
            else:
                finish(b - 2, 3)
            if not started:
                gather(("v", b + 1), 0)
            add_bias_k(b, 3)
            if not started:
                gather(("v", b + 1), 1)
            combine(b - 1, 0)
            project("k", b + 1, 0)
            bind(b, 1)
            combine(b - 1, 1)
            project("k", b + 1, 1)
            bind(b, 2)
            combine(b - 1, 2)
            bind(b, 3)
            gather(("k", b + 2), 0)
            gather(("k", b + 2), 1)

        last = CHUNKS - 1
        if last - 2 in SHARED:
            finish_on_gpsimd(last - 2, 3)
        regroup_on_gpsimd(last, P, HALF)
        regroup(nc.scalar.copy, last, 0, P)
        finish(last - 1, 0)
        combine(last - 1, 3)
        finish(last - 1, 1)
        packed_tiles(("p", last))
        quantise_rows(("p", last), 0, HALF)
        combine(last, 0)
        combine(last, 1)
        regroup(nc.scalar.copy, last, HALF, BLOCK)
        finish(last - 1, 2)
        quantise_rows(("p", last), HALF, BLOCK)
        finish(last - 1, 3)
        combine(last, 2)
        combine(last, 3)
        for i in range(TILES - 1):
            finish(last, i)
        finish_columns(last, TILES - 1, 0, WIDTH // 2)
        finish_columns(last, TILES - 1, WIDTH // 2, WIDTH)
